import numpy as np
import ml_dtypes


def mxq(x, axis, fmt="e4m3"):
    dtype, down = {"e4m3": (ml_dtypes.float8_e4m3fn, 7), "e5m2": (ml_dtypes.float8_e5m2, 14)}[fmt]
    v = np.moveaxis(np.asarray(x, np.float32).astype(ml_dtypes.bfloat16).astype(np.float64), axis, -1)
    blocks = v.reshape(v.shape[:-1] + (-1, 32))
    amax = np.abs(blocks).max(-1, keepdims=True)
    byte = np.maximum(np.where(amax > 0, np.frexp(amax)[1] - 1 + 127, 0) - down, 1)
    scale = np.exp2(byte - 127.0)
    codes = (blocks / scale).astype(np.float32).astype(dtype).astype(np.float64)
    return np.moveaxis((codes * scale).reshape(v.shape), -1, axis)


WIDE = False


def mx_kscale(k):
    if not WIDE:
        return np.ones(k)
    levels = np.array([10, -10, 5, -5, 0])
    a = np.random.permutation(np.resize(levels, k // 512 * 4)).reshape(k // 512, 4)
    idx = np.arange(k)
    return np.exp2(a[idx // 512, idx % 128 // 32])


BF16 = ml_dtypes.bfloat16


def bf(x):
    return np.asarray(x, np.float32).astype(BF16)


def f64(x):
    return np.asarray(x).astype(np.float64)


B, CIN, P, COUT, W, H, HEADS = 2, 1024, 512, 512, 16, 8, 4
N = W * H
EPS = 1e-5


def bn(y, g, b, m, v):
    return (y - f64(m)[None, :, None]) * (f64(g) / np.sqrt(f64(v) + EPS))[None, :, None] + f64(b)[None, :, None]


def setup_inputs():
    s, t = mx_kscale(P), mx_kscale(CIN)
    return {
        "h_attn": bf(np.maximum(np.random.standard_normal((B, P, N)), 0.0) * s[None, :, None]),
        "x": bf(np.random.standard_normal((B, CIN, N)) * t[None, :, None]),
        "conv3_w": bf(np.random.standard_normal((COUT, P)) * 1.5 / np.sqrt(P) / s[None, :]),
        "bn3_g": bf(np.random.uniform(0.5, 1.5, COUT)),
        "bn3_b": bf(np.random.standard_normal(COUT) * 0.3),
        "bn3_m": bf(np.random.standard_normal(COUT) * 0.3),
        "bn3_v": bf(np.random.uniform(0.5, 1.5, COUT)),
        "sc_w": bf(np.random.standard_normal((COUT, CIN)) / np.sqrt(CIN) / t[None, :]),
        "sc_b": bf(np.random.standard_normal(COUT) * 0.3),
        "scbn_g": bf(np.random.uniform(0.5, 1.5, COUT)),
        "scbn_b": bf(np.random.standard_normal(COUT) * 0.3),
        "scbn_m": bf(np.random.standard_normal(COUT) * 0.3),
        "scbn_v": bf(np.random.uniform(0.5, 1.5, COUT)),
    }


def reference(h_attn, x, conv3_w, bn3_g, bn3_b, bn3_m, bn3_v, sc_w, sc_b, scbn_g, scbn_b, scbn_m, scbn_v):
    main = bn(mxq(f64(conv3_w), 1, "e4m3") @ mxq(f64(h_attn), 1, "e4m3"), bn3_g, bn3_b, bn3_m, bn3_v)
    short = (mxq(f64(sc_w), 1, "e4m3") @ mxq(f64(x), 1, "e4m3")) + f64(sc_b)[None, :, None]
    short = bn(short, scbn_g, scbn_b, scbn_m, scbn_v)
    return np.maximum(main + short, 0.0)

@@ -1,0 +1,167 @@
+import concourse.mybir as mybir
+from concourse.masks import make_identity
+
+F32 = mybir.dt.float32
+BF16 = mybir.dt.bfloat16
+U32 = mybir.dt.uint32
+U8 = mybir.dt.uint8
+FP8X4 = mybir.dt.float8_e4m3fn_x4
+ALU = mybir.AluOpType
+ACT = mybir.ActivationFunctionType
+
+P = 128
+BATCH = 2
+POS = 128
+COLS = BATCH * POS
+COUT = 512
+K_MAIN = 512
+K_SHORT = 1024
+PACK = 4
+K_PASS = P * PACK
+R = COUT // P
+EPS = 1e-5
+
+FLOPS = 2 * BATCH * POS * COUT * (K_MAIN + K_SHORT)
+
+
+def tile_bottleneck_transformer_pb_s_kernel(
+    tc, h_attn, x, conv3_w, bn3_g, bn3_b, bn3_m, bn3_v, sc_w, sc_b, scbn_g, scbn_b, scbn_m, scbn_v, out
+):
+    nc = tc.nc
+    with tc.tile_pool(name="keep", bufs=1) as keep, tc.psum_pool(name="psum", bufs=8) as psum:
+        identity = keep.tile([P, P], F32)
+        make_identity(nc, identity[:])
+        one = keep.tile([P, 1], F32)
+        nc.vector.memset(one[:], 1.0)
+        one_root = keep.tile([P, 1], F32)
+        nc.scalar.activation(out=one_root[:], in_=one[:], func=ACT.Sqrt)
+
+        V, G, M, SHIFT, SC_B = 0, 2, 4, 6, 8
+        vectors = [bn3_v, scbn_v, bn3_g, scbn_g, bn3_m, scbn_m, bn3_b, scbn_b, sc_b]
+        bn_raw = keep.tile([P, len(vectors), 16], BF16)
+
+        def load_vector(queue, i):
+            queue.dma_start(out=bn_raw[:, i, 0:R], in_=vectors[i].rearrange("(p r) -> p r", r=R))
+
+        conv3_chunks = conv3_w.rearrange("(p j r) k -> j p (r k)", j=2, r=2)
+        sc_chunks = sc_w.rearrange("(p r) k -> r p k", r=R)
+        w_views = [conv3_chunks[0], conv3_chunks[1]] + [sc_chunks[r] for r in range(R)]
+        N_CHUNKS = len(w_views)
+        w_raw = [keep.tile([P, 2 * K_PASS], BF16, name="w_raw%d" % c) for c in range(N_CHUNKS)]
+        h_raw = keep.tile([P, BATCH, PACK, POS], BF16)
+        x_raw = [keep.tile([P, 2, PACK, POS], BF16, name="x_raw%d" % b) for b in range(BATCH)]
+
+        for i in range(5):
+            load_vector(nc.scalar, i)
+        nc.sync.dma_start(out=w_raw[0][:], in_=w_views[0])
+        nc.sync.dma_start(out=w_raw[1][:], in_=w_views[1])
+        nc.sync.dma_start(
+            out=h_raw[:].rearrange("p b t n -> p b (t n)"), in_=h_attn.rearrange("b (p t) n -> p b (t n)", t=PACK)
+        )
+        for b in range(BATCH):
+            nc.sync.dma_start(
+                out=x_raw[b][:].rearrange("p g t n -> p g (t n)"),
+                in_=x[b].rearrange("(g p t) n -> p g (t n)", g=2, t=PACK),
+            )
+        for i in range(5, len(vectors)):
+            load_vector(nc.sync, i)
+        for c in range(2, N_CHUNKS):
+            nc.sync.dma_start(out=w_raw[c][:], in_=w_views[c])
+
+        w_grouped = [keep.tile([P, 2 * K_PASS], BF16, name="w_grouped%d" % c, align_bytes=64) for c in range(N_CHUNKS)]
+        w_codes = [keep.tile([P, 2 * P], U32, name="w_codes%d" % c, align_bytes=64) for c in range(N_CHUNKS)]
+        w_scales = [keep.tile([P, 2 * P], U8, name="w_scales%d" % c, align_bytes=64) for c in range(N_CHUNKS)]
+
+        def quantise_w(c):
+            words = w_raw[c][:].bitcast(F32).rearrange("p (v q u) -> p v u q", v=2, u=2)
+            bank = psum.tile([P, 2, 2, P], F32, tag="bank")
+            for v in range(2):
+                for u in range(2):
+                    nc.tensor.transpose(bank[:, v, u, :], words[:, v, u, :], identity[:])
+            nc.scalar.copy(
+                out=w_grouped[c][:].bitcast(F32).rearrange("p (v c u) -> p v c u", v=2, u=2),
+                in_=bank[:].rearrange("p v u c -> p v c u"),
+            )
+            nc.vector.quantize_mx(out=w_codes[c][:].bitcast(FP8X4), scales=w_scales[c][:], in_=w_grouped[c][:])
+
+        def weights(c, v):
+            cols = slice(v * P, (v + 1) * P)
+            return {"lhsT": w_codes[c][:, cols].bitcast(FP8X4), "lhsT_scale": w_scales[c][:, cols]}
+
+        quantise_w(0)
+        quantise_w(1)
+
+        h_grouped = keep.tile([P, BATCH, POS, PACK], BF16, align_bytes=64)
+        h_codes = keep.tile([P, COLS], U32, align_bytes=64)
+        h_scales = keep.tile([P, COLS], U8, align_bytes=64)
+        nc.vector.tensor_copy(out=h_grouped[:], in_=h_raw[:].rearrange("p b t n -> p b n t"))
+        nc.vector.quantize_mx(
+            out=h_codes[:].bitcast(FP8X4), scales=h_scales[:], in_=h_grouped[:].rearrange("p b n t -> p (b n t)")
+        )
+
+        var_eps = keep.tile([P, 2, R], F32)
+        nc.vector.tensor_scalar(
+            out=var_eps[:], in0=bn_raw[:, V : V + 2, 0:R], scalar1=EPS, scalar2=None, op0=ALU.add
+        )
+        std = keep.tile([P, 2, R], F32)
+        nc.scalar.activation(out=std[:], in_=var_eps[:], func=ACT.Sqrt)
+        rstd = keep.tile([P, 2, R], F32)
+        nc.vector.reciprocal(out=rstd[:], in_=std[:])
+        scale = keep.tile([P, 2, R], F32)
+        nc.vector.tensor_tensor(out=scale[:], in0=bn_raw[:, G : G + 2, 0:R], in1=rstd[:], op=ALU.mult)
+        mean = keep.tile([P, 2, R], F32)
+        nc.vector.tensor_copy(out=mean[:, 0, :], in_=bn_raw[:, M, 0:R])
+        nc.vector.tensor_tensor(
+            out=mean[:, 1, :], in0=bn_raw[:, M + 1, 0:R], in1=bn_raw[:, SC_B, 0:R], op=ALU.subtract
+        )
+        scaled_mean = keep.tile([P, 2, R], F32)
+        nc.vector.tensor_tensor(out=scaled_mean[:], in0=mean[:], in1=scale[:], op=ALU.mult)
+        shift = keep.tile([P, 2, R], F32)
+        nc.vector.tensor_tensor(
+            out=shift[:], in0=bn_raw[:, SHIFT : SHIFT + 2, 0:R], in1=scaled_mean[:], op=ALU.subtract
+        )
+        bias = keep.tile([P, R], F32)
+        nc.vector.tensor_tensor(out=bias[:], in0=shift[:, 0, :], in1=shift[:, 1, :], op=ALU.add)
+
+        main_term = keep.tile([P, R, COLS], F32)
+        for j in range(2):
+            bank = psum.tile([P, 2, COLS], F32, tag="bank")
+            for v in range(2):
+                nc.tensor.matmul_mx(
+                    out=bank[:, v, :], rhs=h_codes[:].bitcast(FP8X4), rhs_scale=h_scales[:], start=True, stop=True,
+                    **weights(j, v)
+                )
+            for v in range(2):
+                r = 2 * j + v
+                nc.scalar.activation(
+                    out=main_term[:, r, :], in_=bank[:, v, :], func=ACT.Identity,
+                    scale=scale[:, 0, r : r + 1], bias=bias[:, r : r + 1],
+                )
+
+        x_grouped = keep.tile([P, 2, BATCH, POS, PACK], BF16, align_bytes=64)
+        x_codes = keep.tile([P, 2 * COLS], U32, align_bytes=64)
+        x_scales = keep.tile([P, 2 * COLS], U8, align_bytes=64)
+        for b in range(BATCH):
+            nc.vector.tensor_copy(out=x_grouped[:, :, b, :, :], in_=x_raw[b][:].rearrange("p g t n -> p g n t"))
+        nc.vector.quantize_mx(
+            out=x_codes[:].bitcast(FP8X4), scales=x_scales[:], in_=x_grouped[:].rearrange("p g b n t -> p (g b n t)")
+        )
+        for r in range(R):
+            quantise_w(2 + r)
+
+        result = keep.tile([P, R, COLS], F32)
+        out_by_r = out.rearrange("b (p r) n -> r p b n", r=R)
+        for r in range(R):
+            bank = psum.tile([P, COLS], F32, tag="bank")
+            for g in range(2):
+                cols = slice(g * COLS, (g + 1) * COLS)
+                nc.tensor.matmul_mx(
+                    out=bank[:], rhs=x_codes[:, cols].bitcast(FP8X4), rhs_scale=x_scales[:, cols],
+                    start=(g == 0), stop=(g == 1), **weights(2 + r, g)
+                )
+            nc.vector.scalar_tensor_tensor(
+                out=result[:, r, :], in0=bank[:], scalar=scale[:, 1, r : r + 1], in1=main_term[:, r, :],
+                op0=ALU.mult, op1=ALU.add,
+            )
+            nc.scalar.activation(out=result[:, r, :], in_=result[:, r, :], func=ACT.Relu)
+            nc.sync.dma_start(out=out_by_r[r], in_=result[:, r, :].rearrange("p (b n) -> p b n", b=BATCH))

@@ -28,140 +28,172 @@ def tile_bottleneck_transformer_pb_s_kernel(
     tc, h_attn, x, conv3_w, bn3_g, bn3_b, bn3_m, bn3_v, sc_w, sc_b, scbn_g, scbn_b, scbn_m, scbn_v, out
 ):
     nc = tc.nc
-    with tc.tile_pool(name="keep", bufs=1) as keep, tc.psum_pool(name="psum", bufs=8) as psum:
+    with tc.tile_pool(name="keep", bufs=1) as keep, tc.psum_pool(name="psum", bufs=8) as psum, tc.manual_schedule():
+        conv3_raw = keep.tile([P, R, K_MAIN], BF16)
+        sc01_raw = keep.tile([P, 2, K_SHORT], BF16)
+        sc2_raw = keep.tile([P, K_SHORT], BF16)
+        sc3_raw = [keep.tile([P, K_PASS], BF16, name="sc3_raw%d" % g) for g in range(2)]
+        sc_rows = sc_w.rearrange("(p r) k -> p r k", r=R)
+        h_raw = keep.tile([P, BATCH, PACK, POS], BF16)
+        x_raw = keep.tile([P, BATCH, 2, PACK, POS], BF16)
+        vectors = [bn3_v, scbn_v, bn3_g, bn3_m, bn3_b, scbn_g, scbn_m, scbn_b, sc_b]
+        vec_raw = keep.tile([P, len(vectors), 16], BF16)
+        v_both = vec_raw[:, 0:2, 0:R]
+        g3, m3, b3, gsc, msc, bsc, csc = [vec_raw[:, i, 0:R] for i in range(2, len(vectors))]
+        EARLY = 5
+
+        def load_vectors(first, last):
+            for i in range(first, last):
+                nc.sync.dma_start(out=vec_raw[:, i, 0:R], in_=vectors[i].rearrange("(p r) -> p r", r=R))
+
+        nc.sync.dma_start(out=conv3_raw[:], in_=conv3_w.rearrange("(p r) k -> p r k", r=R))
+        nc.sync.dma_start(
+            out=h_raw[:].rearrange("p b t n -> p b (t n)"), in_=h_attn.rearrange("b (p t) n -> p b (t n)", t=PACK)
+        )
+        nc.sync.dma_start(
+            out=x_raw[:].rearrange("p b g t n -> p b g (t n)"),
+            in_=x.rearrange("b (g p t) n -> p b g (t n)", g=2, t=PACK),
+        )
+        load_vectors(0, EARLY)
+        nc.sync.dma_start(out=sc01_raw[:], in_=sc_rows[:, 0:2, :])
+        nc.sync.dma_start(out=sc2_raw[:], in_=sc_rows[:, 2, :])
+        for g in range(2):
+            nc.sync.dma_start(out=sc3_raw[g][:], in_=sc_rows[:, 3, g * K_PASS : (g + 1) * K_PASS])
+        load_vectors(EARLY, len(vectors))
+
         identity = keep.tile([P, P], F32)
         make_identity(nc, identity[:])
         one = keep.tile([P, 1], F32)
         nc.vector.memset(one[:], 1.0)
+        eps = keep.tile([P, 1], F32)
+        nc.vector.memset(eps[:], EPS)
         one_root = keep.tile([P, 1], F32)
         nc.scalar.activation(out=one_root[:], in_=one[:], func=ACT.Sqrt)
 
-        V, G, M, SHIFT, SC_B = 0, 2, 4, 6, 8
-        vectors = [bn3_v, scbn_v, bn3_g, scbn_g, bn3_m, scbn_m, bn3_b, scbn_b, sc_b]
-        bn_raw = keep.tile([P, len(vectors), 16], BF16)
+        pieces = []
+        stationary = {}
 
-        def load_vector(queue, i):
-            queue.dma_start(out=bn_raw[:, i, 0:R], in_=vectors[i].rearrange("(p r) -> p r", r=R))
+        def new_piece(raw, keys):
+            i = len(pieces)
+            units = len(keys)
+            grouped = keep.tile([P, units * K_PASS], BF16, name="w_grouped%d" % i, align_bytes=64)
+            codes = keep.tile([P, units * P], U32, name="w_codes%d" % i, align_bytes=64)
+            scales = keep.tile([P, units * P], U8, name="w_scales%d" % i, align_bytes=64)
+            for v, key in enumerate(keys):
+                cols = slice(v * P, (v + 1) * P)
+                stationary[key] = {"lhsT": codes[:, cols].bitcast(FP8X4), "lhsT_scale": scales[:, cols]}
+            pieces.append((raw, units, grouped, codes, scales))
 
-        conv3_chunks = conv3_w.rearrange("(p j r) k -> j p (r k)", j=2, r=2)
-        sc_chunks = sc_w.rearrange("(p r) k -> r p k", r=R)
-        w_views = [conv3_chunks[0], conv3_chunks[1]] + [sc_chunks[r] for r in range(R)]
-        N_CHUNKS = len(w_views)
-        w_raw = [keep.tile([P, 2 * K_PASS], BF16, name="w_raw%d" % c) for c in range(N_CHUNKS)]
-        h_raw = keep.tile([P, BATCH, PACK, POS], BF16)
-        x_raw = [keep.tile([P, 2, PACK, POS], BF16, name="x_raw%d" % b) for b in range(BATCH)]
+        new_piece(conv3_raw[:, 0:2, :].rearrange("p r k -> p (r k)"), [("main", 0, 0), ("main", 1, 0)])
+        new_piece(conv3_raw[:, 2:4, :].rearrange("p r k -> p (r k)"), [("main", 2, 0), ("main", 3, 0)])
+        new_piece(sc01_raw[:, 0, :], [("short", 0, 0), ("short", 0, 1)])
+        new_piece(sc01_raw[:, 1, :], [("short", 1, 0), ("short", 1, 1)])
+        new_piece(sc2_raw[:], [("short", 2, 0), ("short", 2, 1)])
+        new_piece(sc3_raw[0][:], [("short", 3, 0)])
+        new_piece(sc3_raw[1][:], [("short", 3, 1)])
 
-        for i in range(5):
-            load_vector(nc.scalar, i)
-        nc.sync.dma_start(out=w_raw[0][:], in_=w_views[0])
-        nc.sync.dma_start(out=w_raw[1][:], in_=w_views[1])
-        nc.sync.dma_start(
-            out=h_raw[:].rearrange("p b t n -> p b (t n)"), in_=h_attn.rearrange("b (p t) n -> p b (t n)", t=PACK)
-        )
-        for b in range(BATCH):
-            nc.sync.dma_start(
-                out=x_raw[b][:].rearrange("p g t n -> p g (t n)"),
-                in_=x[b].rearrange("(g p t) n -> p g (t n)", g=2, t=PACK),
-            )
-        for i in range(5, len(vectors)):
-            load_vector(nc.sync, i)
-        for c in range(2, N_CHUNKS):
-            nc.sync.dma_start(out=w_raw[c][:], in_=w_views[c])
-
-        w_grouped = [keep.tile([P, 2 * K_PASS], BF16, name="w_grouped%d" % c, align_bytes=64) for c in range(N_CHUNKS)]
-        w_codes = [keep.tile([P, 2 * P], U32, name="w_codes%d" % c, align_bytes=64) for c in range(N_CHUNKS)]
-        w_scales = [keep.tile([P, 2 * P], U8, name="w_scales%d" % c, align_bytes=64) for c in range(N_CHUNKS)]
-
-        def quantise_w(c):
-            words = w_raw[c][:].bitcast(F32).rearrange("p (v q u) -> p v u q", v=2, u=2)
-            bank = psum.tile([P, 2, 2, P], F32, tag="bank")
-            for v in range(2):
+        def transpose_piece(i):
+            raw, units, grouped, codes, scales = pieces[i]
+            words = raw.bitcast(F32).rearrange("p (v q u) -> p v u q", v=units, u=2)
+            bank = psum.tile([P, units, 2, P], F32, tag="bank")
+            for v in range(units):
                 for u in range(2):
                     nc.tensor.transpose(bank[:, v, u, :], words[:, v, u, :], identity[:])
             nc.scalar.copy(
-                out=w_grouped[c][:].bitcast(F32).rearrange("p (v c u) -> p v c u", v=2, u=2),
+                out=grouped[:].bitcast(F32).rearrange("p (v c u) -> p v c u", v=units, u=2),
                 in_=bank[:].rearrange("p v u c -> p v c u"),
             )
-            nc.vector.quantize_mx(out=w_codes[c][:].bitcast(FP8X4), scales=w_scales[c][:], in_=w_grouped[c][:])
 
-        def weights(c, v):
-            cols = slice(v * P, (v + 1) * P)
-            return {"lhsT": w_codes[c][:, cols].bitcast(FP8X4), "lhsT_scale": w_scales[c][:, cols]}
+        def quantise_piece(i):
+            raw, units, grouped, codes, scales = pieces[i]
+            nc.vector.quantize_mx(out=codes[:].bitcast(FP8X4), scales=scales[:], in_=grouped[:])
 
-        quantise_w(0)
-        quantise_w(1)
+        def small(name):
+            return keep.tile([P, R], F32, name=name)
+
+        def fold(rstd, g, m, b, name):
+            scale = small(name + "_scale")
+            nc.vector.tensor_tensor(out=scale[:], in0=g, in1=rstd, op=ALU.mult)
+            scaled_mean = small(name + "_scaled_mean")
+            nc.vector.tensor_tensor(out=scaled_mean[:], in0=m, in1=scale[:], op=ALU.mult)
+            shift = small(name + "_shift")
+            nc.vector.tensor_tensor(out=shift[:], in0=b, in1=scaled_mean[:], op=ALU.subtract)
+            return scale, shift
 
         h_grouped = keep.tile([P, BATCH, POS, PACK], BF16, align_bytes=64)
         h_codes = keep.tile([P, COLS], U32, align_bytes=64)
         h_scales = keep.tile([P, COLS], U8, align_bytes=64)
-        nc.vector.tensor_copy(out=h_grouped[:], in_=h_raw[:].rearrange("p b t n -> p b n t"))
-        nc.vector.quantize_mx(
-            out=h_codes[:].bitcast(FP8X4), scales=h_scales[:], in_=h_grouped[:].rearrange("p b n t -> p (b n t)")
-        )
-
-        var_eps = keep.tile([P, 2, R], F32)
-        nc.vector.tensor_scalar(
-            out=var_eps[:], in0=bn_raw[:, V : V + 2, 0:R], scalar1=EPS, scalar2=None, op0=ALU.add
-        )
-        std = keep.tile([P, 2, R], F32)
-        nc.scalar.activation(out=std[:], in_=var_eps[:], func=ACT.Sqrt)
-        rstd = keep.tile([P, 2, R], F32)
-        nc.vector.reciprocal(out=rstd[:], in_=std[:])
-        scale = keep.tile([P, 2, R], F32)
-        nc.vector.tensor_tensor(out=scale[:], in0=bn_raw[:, G : G + 2, 0:R], in1=rstd[:], op=ALU.mult)
-        mean = keep.tile([P, 2, R], F32)
-        nc.vector.tensor_copy(out=mean[:, 0, :], in_=bn_raw[:, M, 0:R])
-        nc.vector.tensor_tensor(
-            out=mean[:, 1, :], in0=bn_raw[:, M + 1, 0:R], in1=bn_raw[:, SC_B, 0:R], op=ALU.subtract
-        )
-        scaled_mean = keep.tile([P, 2, R], F32)
-        nc.vector.tensor_tensor(out=scaled_mean[:], in0=mean[:], in1=scale[:], op=ALU.mult)
-        shift = keep.tile([P, 2, R], F32)
-        nc.vector.tensor_tensor(
-            out=shift[:], in0=bn_raw[:, SHIFT : SHIFT + 2, 0:R], in1=scaled_mean[:], op=ALU.subtract
-        )
-        bias = keep.tile([P, R], F32)
-        nc.vector.tensor_tensor(out=bias[:], in0=shift[:, 0, :], in1=shift[:, 1, :], op=ALU.add)
-
+        x_grouped = keep.tile([P, 2, BATCH, POS, PACK], BF16, align_bytes=64)
+        x_codes = keep.tile([P, 2 * COLS], U32, align_bytes=64)
+        x_scales = keep.tile([P, 2 * COLS], U8, align_bytes=64)
         main_term = keep.tile([P, R, COLS], F32)
-        for j in range(2):
+        summed = keep.tile([P, R, COLS], F32)
+        result = keep.tile([P, R, COLS], F32)
+        out_by_r = out.rearrange("b (p r) n -> r p b n", r=R)
+
+        def main_branch(j):
             bank = psum.tile([P, 2, COLS], F32, tag="bank")
             for v in range(2):
                 nc.tensor.matmul_mx(
                     out=bank[:, v, :], rhs=h_codes[:].bitcast(FP8X4), rhs_scale=h_scales[:], start=True, stop=True,
-                    **weights(j, v)
+                    **stationary[("main", 2 * j + v, 0)]
                 )
             for v in range(2):
                 r = 2 * j + v
                 nc.scalar.activation(
                     out=main_term[:, r, :], in_=bank[:, v, :], func=ACT.Identity,
-                    scale=scale[:, 0, r : r + 1], bias=bias[:, r : r + 1],
+                    scale=scale3[:, r : r + 1], bias=shift3[:, r : r + 1],
                 )
 
-        x_grouped = keep.tile([P, 2, BATCH, POS, PACK], BF16, align_bytes=64)
-        x_codes = keep.tile([P, 2 * COLS], U32, align_bytes=64)
-        x_scales = keep.tile([P, 2 * COLS], U8, align_bytes=64)
-        for b in range(BATCH):
-            nc.vector.tensor_copy(out=x_grouped[:, :, b, :, :], in_=x_raw[b][:].rearrange("p g t n -> p g n t"))
-        nc.vector.quantize_mx(
-            out=x_codes[:].bitcast(FP8X4), scales=x_scales[:], in_=x_grouped[:].rearrange("p g b n t -> p (g b n t)")
-        )
-        for r in range(R):
-            quantise_w(2 + r)
-
-        result = keep.tile([P, R, COLS], F32)
-        out_by_r = out.rearrange("b (p r) n -> r p b n", r=R)
-        for r in range(R):
+        def finish(r):
             bank = psum.tile([P, COLS], F32, tag="bank")
             for g in range(2):
                 cols = slice(g * COLS, (g + 1) * COLS)
                 nc.tensor.matmul_mx(
                     out=bank[:], rhs=x_codes[:, cols].bitcast(FP8X4), rhs_scale=x_scales[:, cols],
-                    start=(g == 0), stop=(g == 1), **weights(2 + r, g)
+                    start=(g == 0), stop=(g == 1), **stationary[("short", r, g)]
                 )
             nc.vector.scalar_tensor_tensor(
-                out=result[:, r, :], in0=bank[:], scalar=scale[:, 1, r : r + 1], in1=main_term[:, r, :],
+                out=summed[:, r, :], in0=bank[:], scalar=scalesc[:, r : r + 1], in1=main_term[:, r, :],
                 op0=ALU.mult, op1=ALU.add,
             )
-            nc.scalar.activation(out=result[:, r, :], in_=result[:, r, :], func=ACT.Relu)
+            nc.scalar.activation(out=result[:, r, :], in_=summed[:, r, :], func=ACT.Relu, bias=shiftsc[:, r : r + 1])
             nc.sync.dma_start(out=out_by_r[r], in_=result[:, r, :].rearrange("p (b n) -> p b n", b=BATCH))
+
+        def regroup_x(engine_copy, g):
+            engine_copy(out=x_grouped[:, g, :, :, :], in_=x_raw[:, :, g, :, :].rearrange("p b t n -> p b n t"))
+
+        transpose_piece(0)
+        transpose_piece(1)
+        nc.vector.tensor_copy(out=h_grouped[:], in_=h_raw[:].rearrange("p b t n -> p b n t"))
+        quantise_piece(0)
+        nc.vector.quantize_mx(
+            out=h_codes[:].bitcast(FP8X4), scales=h_scales[:], in_=h_grouped[:].rearrange("p b n t -> p (b n t)")
+        )
+        quantise_piece(1)
+        std = keep.tile([P, 2, R], F32)
+        nc.scalar.activation(out=std[:], in_=v_both, func=ACT.Sqrt, bias=eps[:])
+        rstd = keep.tile([P, 2, R], F32)
+        nc.vector.reciprocal(out=rstd[:], in_=std[:])
+        scale3, shift3 = fold(rstd[:, 0, :], g3, m3, b3, "bn3")
+        main_branch(0)
+        main_branch(1)
+        regroup_x(nc.vector.tensor_copy, 0)
+        regroup_x(nc.vector.tensor_copy, 1)
+        for i in range(2, len(pieces)):
+            transpose_piece(i)
+        nc.vector.quantize_mx(
+            out=x_codes[:].bitcast(FP8X4), scales=x_scales[:], in_=x_grouped[:].rearrange("p g b n t -> p (g b n t)")
+        )
+        quantise_piece(2)
+        quantise_piece(3)
+        mean_less_bias = small("mean_less_bias")
+        nc.vector.tensor_tensor(out=mean_less_bias[:], in0=msc, in1=csc, op=ALU.subtract)
+        scalesc, shiftsc = fold(rstd[:, 1, :], gsc, mean_less_bias[:], bsc, "scbn")
+        quantise_piece(4)
+        finish(0)
+        quantise_piece(5)
+        quantise_piece(6)
+        finish(1)
+        finish(2)
+        finish(3)

@@ -30,8 +30,7 @@ def tile_bottleneck_transformer_pb_s_kernel(
     nc = tc.nc
     with tc.tile_pool(name="keep", bufs=1) as keep, tc.psum_pool(name="psum", bufs=8) as psum, tc.manual_schedule():
         conv3_raw = keep.tile([P, R, K_MAIN], BF16)
-        sc01_raw = keep.tile([P, 2, K_SHORT], BF16)
-        sc2_raw = keep.tile([P, K_SHORT], BF16)
+        sc_raw = [keep.tile([P, K_SHORT], BF16, name="sc_raw%d" % r) for r in range(R - 1)]
         sc3_raw = [keep.tile([P, K_PASS], BF16, name="sc3_raw%d" % g) for g in range(2)]
         sc_rows = sc_w.rearrange("(p r) k -> p r k", r=R)
         h_raw = keep.tile([P, BATCH, PACK, POS], BF16)
@@ -50,13 +49,14 @@ def tile_bottleneck_transformer_pb_s_kernel(
         nc.sync.dma_start(
             out=h_raw[:].rearrange("p b t n -> p b (t n)"), in_=h_attn.rearrange("b (p t) n -> p b (t n)", t=PACK)
         )
+        load_vectors(0, EARLY)
+        nc.sync.dma_start(out=sc_raw[0][:], in_=sc_rows[:, 0, :])
         nc.sync.dma_start(
             out=x_raw[:].rearrange("p b g t n -> p b g (t n)"),
             in_=x.rearrange("b (g p t) n -> p b g (t n)", g=2, t=PACK),
         )
-        load_vectors(0, EARLY)
-        nc.sync.dma_start(out=sc01_raw[:], in_=sc_rows[:, 0:2, :])
-        nc.sync.dma_start(out=sc2_raw[:], in_=sc_rows[:, 2, :])
+        nc.sync.dma_start(out=sc_raw[1][:], in_=sc_rows[:, 1, :])
+        nc.sync.dma_start(out=sc_raw[2][:], in_=sc_rows[:, 2, :])
         for g in range(2):
             nc.sync.dma_start(out=sc3_raw[g][:], in_=sc_rows[:, 3, g * K_PASS : (g + 1) * K_PASS])
         load_vectors(EARLY, len(vectors))
@@ -86,9 +86,8 @@ def tile_bottleneck_transformer_pb_s_kernel(
 
         new_piece(conv3_raw[:, 0:2, :].rearrange("p r k -> p (r k)"), [("main", 0, 0), ("main", 1, 0)])
         new_piece(conv3_raw[:, 2:4, :].rearrange("p r k -> p (r k)"), [("main", 2, 0), ("main", 3, 0)])
-        new_piece(sc01_raw[:, 0, :], [("short", 0, 0), ("short", 0, 1)])
-        new_piece(sc01_raw[:, 1, :], [("short", 1, 0), ("short", 1, 1)])
-        new_piece(sc2_raw[:], [("short", 2, 0), ("short", 2, 1)])
+        for r in range(R - 1):
+            new_piece(sc_raw[r][:], [("short", r, 0), ("short", r, 1)])
         new_piece(sc3_raw[0][:], [("short", 3, 0)])
         new_piece(sc3_raw[1][:], [("short", 3, 1)])
 
@@ -131,13 +130,18 @@ def tile_bottleneck_transformer_pb_s_kernel(
         result = keep.tile([P, R, COLS], F32)
         out_by_r = out.rearrange("b (p r) n -> r p b n", r=R)
 
-        def main_branch(j):
-            bank = psum.tile([P, 2, COLS], F32, tag="bank")
+        main_banks = [psum.tile([P, 2, COLS], F32, tag="bank", name="main_bank%d" % j) for j in range(2)]
+
+        def main_passes(j):
+            bank = main_banks[j]
             for v in range(2):
                 nc.tensor.matmul_mx(
                     out=bank[:, v, :], rhs=h_codes[:].bitcast(FP8X4), rhs_scale=h_scales[:], start=True, stop=True,
                     **stationary[("main", 2 * j + v, 0)]
                 )
+
+        def main_out(j):
+            bank = main_banks[j]
             for v in range(2):
                 r = 2 * j + v
                 nc.scalar.activation(
@@ -176,16 +180,19 @@ def tile_bottleneck_transformer_pb_s_kernel(
         rstd = keep.tile([P, 2, R], F32)
         nc.vector.reciprocal(out=rstd[:], in_=std[:])
         scale3, shift3 = fold(rstd[:, 0, :], g3, m3, b3, "bn3")
-        main_branch(0)
-        main_branch(1)
+        transpose_piece(2)
+        main_passes(0)
+        main_passes(1)
+        main_out(0)
         regroup_x(nc.vector.tensor_copy, 0)
+        quantise_piece(2)
         regroup_x(nc.vector.tensor_copy, 1)
-        for i in range(2, len(pieces)):
-            transpose_piece(i)
         nc.vector.quantize_mx(
             out=x_codes[:].bitcast(FP8X4), scales=x_scales[:], in_=x_grouped[:].rearrange("p g b n t -> p (g b n t)")
         )
-        quantise_piece(2)
+        for i in range(3, len(pieces)):
+            transpose_piece(i)
+        main_out(1)
         quantise_piece(3)
         mean_less_bias = small("mean_less_bias")
         nc.vector.tensor_tensor(out=mean_less_bias[:], in0=msc, in1=csc, op=ALU.subtract)

@@ -28,35 +28,41 @@ def tile_bottleneck_transformer_pb_s_kernel(
     tc, h_attn, x, conv3_w, bn3_g, bn3_b, bn3_m, bn3_v, sc_w, sc_b, scbn_g, scbn_b, scbn_m, scbn_v, out
 ):
     nc = tc.nc
-    with tc.tile_pool(name="keep", bufs=1) as keep, tc.psum_pool(name="psum", bufs=8) as psum, tc.manual_schedule():
-        conv3_raw = keep.tile([P, R, K_MAIN], BF16)
+    with tc.tile_pool(name="keep", bufs=1) as keep, tc.psum_pool(name="psum", bufs=1) as psum, tc.manual_schedule():
+        conv3_rows = conv3_w.rearrange("(p r) k -> p r k", r=R)
+        sc_rows = sc_w.rearrange("(p r) k -> p r k", r=R)
+        conv3_raw = [keep.tile([P, 2, K_MAIN], BF16, name="conv3_raw%d" % j) for j in range(2)]
         sc_raw = [keep.tile([P, K_SHORT], BF16, name="sc_raw%d" % r) for r in range(R - 1)]
         sc3_raw = [keep.tile([P, K_PASS], BF16, name="sc3_raw%d" % g) for g in range(2)]
-        sc_rows = sc_w.rearrange("(p r) k -> p r k", r=R)
         h_raw = keep.tile([P, BATCH, PACK, POS], BF16)
-        x_raw = keep.tile([P, BATCH, 2, PACK, POS], BF16)
-        vectors = [bn3_v, scbn_v, bn3_g, bn3_m, bn3_b, scbn_g, scbn_m, scbn_b, sc_b]
+        x_raw = [keep.tile([P, BATCH, PACK, POS], BF16, name="x_raw%d" % g) for g in range(2)]
+        vectors = [bn3_v, scbn_v, bn3_g, scbn_g, scbn_m, sc_b, bn3_m, bn3_b, scbn_b]
         vec_raw = keep.tile([P, len(vectors), 16], BF16)
         v_both = vec_raw[:, 0:2, 0:R]
-        g3, m3, b3, gsc, msc, bsc, csc = [vec_raw[:, i, 0:R] for i in range(2, len(vectors))]
-        EARLY = 5
+        g_both = vec_raw[:, 2:4, 0:R]
+        msc, csc, m3, b3, bsc = [vec_raw[:, i, 0:R] for i in range(4, len(vectors))]
+        EARLY = 4
 
         def load_vectors(first, last):
             for i in range(first, last):
                 nc.sync.dma_start(out=vec_raw[:, i, 0:R], in_=vectors[i].rearrange("(p r) -> p r", r=R))
 
-        nc.sync.dma_start(out=conv3_raw[:], in_=conv3_w.rearrange("(p r) k -> p r k", r=R))
+        def load_x(g):
+            nc.sync.dma_start(
+                out=x_raw[g][:].rearrange("p b t n -> p b (t n)"),
+                in_=x[:, g * K_PASS : (g + 1) * K_PASS, :].rearrange("b (p t) n -> p b (t n)", t=PACK),
+            )
+
+        nc.sync.dma_start(out=conv3_raw[0][:], in_=conv3_rows[:, 0:2, :])
         nc.sync.dma_start(
             out=h_raw[:].rearrange("p b t n -> p b (t n)"), in_=h_attn.rearrange("b (p t) n -> p b (t n)", t=PACK)
         )
         load_vectors(0, EARLY)
-        nc.sync.dma_start(out=sc_raw[0][:], in_=sc_rows[:, 0, :])
-        nc.sync.dma_start(
-            out=x_raw[:].rearrange("p b g t n -> p b g (t n)"),
-            in_=x.rearrange("b (g p t) n -> p b g (t n)", g=2, t=PACK),
-        )
-        nc.sync.dma_start(out=sc_raw[1][:], in_=sc_rows[:, 1, :])
-        nc.sync.dma_start(out=sc_raw[2][:], in_=sc_rows[:, 2, :])
+        nc.sync.dma_start(out=conv3_raw[1][:], in_=conv3_rows[:, 2:4, :])
+        load_x(0)
+        load_x(1)
+        for r in range(R - 1):
+            nc.sync.dma_start(out=sc_raw[r][:], in_=sc_rows[:, r, :])
         for g in range(2):
             nc.sync.dma_start(out=sc3_raw[g][:], in_=sc_rows[:, 3, g * K_PASS : (g + 1) * K_PASS])
         load_vectors(EARLY, len(vectors))
@@ -70,31 +76,31 @@ def tile_bottleneck_transformer_pb_s_kernel(
         one_root = keep.tile([P, 1], F32)
         nc.scalar.activation(out=one_root[:], in_=one[:], func=ACT.Sqrt)
 
-        pieces = []
+        pieces = {}
         stationary = {}
 
-        def new_piece(raw, keys):
-            i = len(pieces)
+        def new_piece(name, raw, keys, bank):
             units = len(keys)
-            grouped = keep.tile([P, units * K_PASS], BF16, name="w_grouped%d" % i, align_bytes=64)
-            codes = keep.tile([P, units * P], U32, name="w_codes%d" % i, align_bytes=64)
-            scales = keep.tile([P, units * P], U8, name="w_scales%d" % i, align_bytes=64)
+            grouped = keep.tile([P, units * K_PASS], BF16, name="w_grouped_" + name, align_bytes=64)
+            codes = keep.tile([P, units * P], U32, name="w_codes_" + name, align_bytes=64)
+            scales = keep.tile([P, units * P], U8, name="w_scales_" + name, align_bytes=64)
             for v, key in enumerate(keys):
                 cols = slice(v * P, (v + 1) * P)
                 stationary[key] = {"lhsT": codes[:, cols].bitcast(FP8X4), "lhsT_scale": scales[:, cols]}
-            pieces.append((raw, units, grouped, codes, scales))
+            pieces[name] = (raw, units, grouped, codes, scales, bank)
 
-        new_piece(conv3_raw[:, 0:2, :].rearrange("p r k -> p (r k)"), [("main", 0, 0), ("main", 1, 0)])
-        new_piece(conv3_raw[:, 2:4, :].rearrange("p r k -> p (r k)"), [("main", 2, 0), ("main", 3, 0)])
-        for r in range(R - 1):
-            new_piece(sc_raw[r][:], [("short", r, 0), ("short", r, 1)])
-        new_piece(sc3_raw[0][:], [("short", 3, 0)])
-        new_piece(sc3_raw[1][:], [("short", 3, 1)])
+        new_piece("c3a", conv3_raw[0][:].rearrange("p r k -> p (r k)"), [("main", 0, 0), ("main", 1, 0)], "t0")
+        new_piece("c3b", conv3_raw[1][:].rearrange("p r k -> p (r k)"), [("main", 2, 0), ("main", 3, 0)], "t1")
+        new_piece("sc0", sc_raw[0][:], [("short", 0, 0), ("short", 0, 1)], "t2")
+        new_piece("sc1", sc_raw[1][:], [("short", 1, 0), ("short", 1, 1)], "t3")
+        new_piece("sc2", sc_raw[2][:], [("short", 2, 0), ("short", 2, 1)], "t0")
+        new_piece("sc3a", sc3_raw[0][:], [("short", 3, 0)], "t1")
+        new_piece("sc3b", sc3_raw[1][:], [("short", 3, 1)], "t2")
 
-        def transpose_piece(i):
-            raw, units, grouped, codes, scales = pieces[i]
+        def transpose_piece(name):
+            raw, units, grouped, codes, scales, bank_tag = pieces[name]
             words = raw.bitcast(F32).rearrange("p (v q u) -> p v u q", v=units, u=2)
-            bank = psum.tile([P, units, 2, P], F32, tag="bank")
+            bank = psum.tile([P, units, 2, P], F32, tag=bank_tag, name="bank_" + name)
             for v in range(units):
                 for u in range(2):
                     nc.tensor.transpose(bank[:, v, u, :], words[:, v, u, :], identity[:])
@@ -103,21 +109,9 @@ def tile_bottleneck_transformer_pb_s_kernel(
                 in_=bank[:].rearrange("p v u c -> p v c u"),
             )
 
-        def quantise_piece(i):
-            raw, units, grouped, codes, scales = pieces[i]
+        def quantise_piece(name):
+            raw, units, grouped, codes, scales, bank_tag = pieces[name]
             nc.vector.quantize_mx(out=codes[:].bitcast(FP8X4), scales=scales[:], in_=grouped[:])
-
-        def small(name):
-            return keep.tile([P, R], F32, name=name)
-
-        def fold(rstd, g, m, b, name):
-            scale = small(name + "_scale")
-            nc.vector.tensor_tensor(out=scale[:], in0=g, in1=rstd, op=ALU.mult)
-            scaled_mean = small(name + "_scaled_mean")
-            nc.vector.tensor_tensor(out=scaled_mean[:], in0=m, in1=scale[:], op=ALU.mult)
-            shift = small(name + "_shift")
-            nc.vector.tensor_tensor(out=shift[:], in0=b, in1=scaled_mean[:], op=ALU.subtract)
-            return scale, shift
 
         h_grouped = keep.tile([P, BATCH, POS, PACK], BF16, align_bytes=64)
         h_codes = keep.tile([P, COLS], U32, align_bytes=64)
@@ -130,77 +124,101 @@ def tile_bottleneck_transformer_pb_s_kernel(
         result = keep.tile([P, R, COLS], F32)
         out_by_r = out.rearrange("b (p r) n -> r p b n", r=R)
 
-        main_banks = [psum.tile([P, 2, COLS], F32, tag="bank", name="main_bank%d" % j) for j in range(2)]
+        def small(name, width=R):
+            return keep.tile([P, width], F32, name=name)
+
+        main_banks = {}
 
         def main_passes(j):
-            bank = main_banks[j]
+            bank = psum.tile([P, 2, COLS], F32, tag="m%d" % j, name="main_bank%d" % j)
+            main_banks[j] = bank
             for v in range(2):
                 nc.tensor.matmul_mx(
                     out=bank[:, v, :], rhs=h_codes[:].bitcast(FP8X4), rhs_scale=h_scales[:], start=True, stop=True,
                     **stationary[("main", 2 * j + v, 0)]
                 )
 
-        def main_out(j):
-            bank = main_banks[j]
-            for v in range(2):
-                r = 2 * j + v
-                nc.scalar.activation(
-                    out=main_term[:, r, :], in_=bank[:, v, :], func=ACT.Identity,
-                    scale=scale3[:, r : r + 1], bias=shift3[:, r : r + 1],
-                )
+        def main_out(r):
+            nc.scalar.activation(
+                out=main_term[:, r, :], in_=main_banks[r // 2][:, r % 2, :], func=ACT.Identity,
+                scale=scale_both[:, 0, r : r + 1],
+            )
 
-        def finish(r):
-            bank = psum.tile([P, COLS], F32, tag="bank")
+        short_banks = {}
+
+        def short_passes(r, bank_tag):
+            bank = psum.tile([P, COLS], F32, tag=bank_tag, name="short_bank%d" % r)
+            short_banks[r] = bank
             for g in range(2):
                 cols = slice(g * COLS, (g + 1) * COLS)
                 nc.tensor.matmul_mx(
                     out=bank[:], rhs=x_codes[:, cols].bitcast(FP8X4), rhs_scale=x_scales[:, cols],
                     start=(g == 0), stop=(g == 1), **stationary[("short", r, g)]
                 )
+
+        def add_branches(r):
             nc.vector.scalar_tensor_tensor(
-                out=summed[:, r, :], in0=bank[:], scalar=scalesc[:, r : r + 1], in1=main_term[:, r, :],
+                out=summed[:, r, :], in0=short_banks[r][:], scalar=scale_both[:, 1, r : r + 1], in1=main_term[:, r, :],
                 op0=ALU.mult, op1=ALU.add,
             )
-            nc.scalar.activation(out=result[:, r, :], in_=summed[:, r, :], func=ACT.Relu, bias=shiftsc[:, r : r + 1])
+
+        def finish(r):
+            nc.scalar.activation(out=result[:, r, :], in_=summed[:, r, :], func=ACT.Relu, bias=shift[:, r : r + 1])
             nc.sync.dma_start(out=out_by_r[r], in_=result[:, r, :].rearrange("p (b n) -> p b n", b=BATCH))
 
-        def regroup_x(engine_copy, g):
-            engine_copy(out=x_grouped[:, g, :, :, :], in_=x_raw[:, :, g, :, :].rearrange("p b t n -> p b n t"))
+        def regroup_x(g):
+            nc.vector.tensor_copy(out=x_grouped[:, g, :, :, :], in_=x_raw[g][:].rearrange("p b t n -> p b n t"))
 
-        transpose_piece(0)
-        transpose_piece(1)
+        transpose_piece("c3a")
         nc.vector.tensor_copy(out=h_grouped[:], in_=h_raw[:].rearrange("p b t n -> p b n t"))
-        quantise_piece(0)
+        std = keep.tile([P, 2, R], F32)
+        nc.scalar.activation(out=std[:], in_=v_both, func=ACT.Sqrt, bias=eps[:])
         nc.vector.quantize_mx(
             out=h_codes[:].bitcast(FP8X4), scales=h_scales[:], in_=h_grouped[:].rearrange("p b n t -> p (b n t)")
         )
-        quantise_piece(1)
-        std = keep.tile([P, 2, R], F32)
-        nc.scalar.activation(out=std[:], in_=v_both, func=ACT.Sqrt, bias=eps[:])
+        quantise_piece("c3a")
         rstd = keep.tile([P, 2, R], F32)
         nc.vector.reciprocal(out=rstd[:], in_=std[:])
-        scale3, shift3 = fold(rstd[:, 0, :], g3, m3, b3, "bn3")
-        transpose_piece(2)
+        scale_both = keep.tile([P, 2, R], F32)
+        nc.vector.tensor_tensor(out=scale_both[:], in0=g_both, in1=rstd[:], op=ALU.mult)
+        transpose_piece("c3b")
         main_passes(0)
-        main_passes(1)
+        regroup_x(0)
+        regroup_x(1)
         main_out(0)
-        regroup_x(nc.vector.tensor_copy, 0)
-        quantise_piece(2)
-        regroup_x(nc.vector.tensor_copy, 1)
+        main_out(1)
+        quantise_piece("c3b")
         nc.vector.quantize_mx(
             out=x_codes[:].bitcast(FP8X4), scales=x_scales[:], in_=x_grouped[:].rearrange("p g b n t -> p (g b n t)")
         )
-        for i in range(3, len(pieces)):
-            transpose_piece(i)
-        main_out(1)
-        quantise_piece(3)
+        for name in ("sc0", "sc1", "sc2", "sc3a", "sc3b"):
+            transpose_piece(name)
+        main_passes(1)
+        main_out(2)
+        main_out(3)
+        quantise_piece("sc0")
+        short_passes(0, "f0")
+        quantise_piece("sc1")
+        short_passes(1, "f1")
         mean_less_bias = small("mean_less_bias")
         nc.vector.tensor_tensor(out=mean_less_bias[:], in0=msc, in1=csc, op=ALU.subtract)
-        scalesc, shiftsc = fold(rstd[:, 1, :], gsc, mean_less_bias[:], bsc, "scbn")
-        quantise_piece(4)
+        scaled_sc = small("scaled_sc")
+        nc.vector.tensor_tensor(out=scaled_sc[:], in0=mean_less_bias[:], in1=scale_both[:, 1, :], op=ALU.mult)
+        scaled_3 = small("scaled_3")
+        nc.vector.tensor_tensor(out=scaled_3[:], in0=m3, in1=scale_both[:, 0, :], op=ALU.mult)
+        shift_3 = small("shift_3")
+        nc.vector.tensor_tensor(out=shift_3[:], in0=b3, in1=scaled_3[:], op=ALU.subtract)
+        shift_less = small("shift_less")
+        nc.vector.tensor_tensor(out=shift_less[:], in0=shift_3[:], in1=scaled_sc[:], op=ALU.subtract)
+        shift = small("shift")
+        nc.vector.tensor_tensor(out=shift[:], in0=bsc, in1=shift_less[:], op=ALU.add)
+        quantise_piece("sc2")
+        short_passes(2, "t3")
+        quantise_piece("sc3a")
+        add_branches(0)
         finish(0)
-        quantise_piece(5)
-        quantise_piece(6)
-        finish(1)
-        finish(2)
-        finish(3)
+        quantise_piece("sc3b")
+        short_passes(3, "m0")
+        for r in range(1, R):
+            add_branches(r)
+            finish(r)

@@ -201,24 +201,22 @@ def tile_bottleneck_transformer_pb_s_kernel(
         quantise_piece("sc1")
         short_passes(1, "f1")
         mean_less_bias = small("mean_less_bias")
-        nc.vector.tensor_tensor(out=mean_less_bias[:], in0=msc, in1=csc, op=ALU.subtract)
+        nc.gpsimd.tensor_tensor(out=mean_less_bias[:], in0=msc, in1=csc, op=ALU.subtract)
         scaled_sc = small("scaled_sc")
-        nc.vector.tensor_tensor(out=scaled_sc[:], in0=mean_less_bias[:], in1=scale_both[:, 1, :], op=ALU.mult)
+        nc.gpsimd.tensor_tensor(out=scaled_sc[:], in0=mean_less_bias[:], in1=scale_both[:, 1, :], op=ALU.mult)
         scaled_3 = small("scaled_3")
-        nc.vector.tensor_tensor(out=scaled_3[:], in0=m3, in1=scale_both[:, 0, :], op=ALU.mult)
+        nc.gpsimd.tensor_tensor(out=scaled_3[:], in0=m3, in1=scale_both[:, 0, :], op=ALU.mult)
         shift_3 = small("shift_3")
-        nc.vector.tensor_tensor(out=shift_3[:], in0=b3, in1=scaled_3[:], op=ALU.subtract)
+        nc.gpsimd.tensor_tensor(out=shift_3[:], in0=b3, in1=scaled_3[:], op=ALU.subtract)
         shift_less = small("shift_less")
-        nc.vector.tensor_tensor(out=shift_less[:], in0=shift_3[:], in1=scaled_sc[:], op=ALU.subtract)
+        nc.gpsimd.tensor_tensor(out=shift_less[:], in0=shift_3[:], in1=scaled_sc[:], op=ALU.subtract)
         shift = small("shift")
-        nc.vector.tensor_tensor(out=shift[:], in0=bsc, in1=shift_less[:], op=ALU.add)
+        nc.gpsimd.tensor_tensor(out=shift[:], in0=bsc, in1=shift_less[:], op=ALU.add)
         quantise_piece("sc2")
         short_passes(2, "t3")
         quantise_piece("sc3a")
-        add_branches(0)
-        finish(0)
         quantise_piece("sc3b")
         short_passes(3, "m0")
-        for r in range(1, R):
+        for r in range(R):
             add_branches(r)
             finish(r)

@@ -43,9 +43,9 @@ def tile_bottleneck_transformer_pb_s_kernel(
         msc, csc, m3, b3, bsc = [vec_raw[:, i, 0:R] for i in range(4, len(vectors))]
         EARLY = 4
 
-        def load_vectors(first, last):
+        def load_vectors(queue, first, last):
             for i in range(first, last):
-                nc.sync.dma_start(out=vec_raw[:, i, 0:R], in_=vectors[i].rearrange("(p r) -> p r", r=R))
+                queue.dma_start(out=vec_raw[:, i, 0:R], in_=vectors[i].rearrange("(p r) -> p r", r=R))
 
         def load_x(g):
             nc.sync.dma_start(
@@ -53,11 +53,11 @@ def tile_bottleneck_transformer_pb_s_kernel(
                 in_=x[:, g * K_PASS : (g + 1) * K_PASS, :].rearrange("b (p t) n -> p b (t n)", t=PACK),
             )
 
+        load_vectors(nc.scalar, 0, EARLY)
         nc.sync.dma_start(out=conv3_raw[0][:], in_=conv3_rows[:, 0:2, :])
         nc.sync.dma_start(
             out=h_raw[:].rearrange("p b t n -> p b (t n)"), in_=h_attn.rearrange("b (p t) n -> p b (t n)", t=PACK)
         )
-        load_vectors(0, EARLY)
         nc.sync.dma_start(out=conv3_raw[1][:], in_=conv3_rows[:, 2:4, :])
         load_x(0)
         load_x(1)
@@ -65,7 +65,7 @@ def tile_bottleneck_transformer_pb_s_kernel(
             nc.sync.dma_start(out=sc_raw[r][:], in_=sc_rows[:, r, :])
         for g in range(2):
             nc.sync.dma_start(out=sc3_raw[g][:], in_=sc_rows[:, 3, g * K_PASS : (g + 1) * K_PASS])
-        load_vectors(EARLY, len(vectors))
+        load_vectors(nc.sync, EARLY, len(vectors))
 
         identity = keep.tile([P, P], F32)
         make_identity(nc, identity[:])

@@ -76,6 +76,15 @@ def tile_bottleneck_transformer_pb_s_kernel(
         one_root = keep.tile([P, 1], F32)
         nc.scalar.activation(out=one_root[:], in_=one[:], func=ACT.Sqrt)
 
+        WARM = 256
+        zeros = keep.tile([P, WARM], F32)
+        nc.vector.memset(zeros[:], 0.0)
+        warm_bank = psum.tile([P, WARM], F32, tag="f1", name="warm_bank")
+
+        def keep_warm(n):
+            for i in range(n):
+                nc.tensor.matmul(warm_bank[:], lhsT=zeros[:, 0:P], rhs=zeros[:], start=True, stop=True)
+
         pieces = {}
         stationary = {}
 
@@ -169,7 +178,9 @@ def tile_bottleneck_transformer_pb_s_kernel(
         def regroup_x(g):
             nc.vector.tensor_copy(out=x_grouped[:, g, :, :, :], in_=x_raw[g][:].rearrange("p b t n -> p b n t"))
 
+        keep_warm(2)
         transpose_piece("c3a")
+        keep_warm(1)
         nc.vector.tensor_copy(out=h_grouped[:], in_=h_raw[:].rearrange("p b t n -> p b n t"))
         std = keep.tile([P, 2, R], F32)
         nc.scalar.activation(out=std[:], in_=v_both, func=ACT.Sqrt, bias=eps[:])
@@ -183,6 +194,7 @@ def tile_bottleneck_transformer_pb_s_kernel(
         nc.vector.tensor_tensor(out=scale_both[:], in0=g_both, in1=rstd[:], op=ALU.mult)
         transpose_piece("c3b")
         main_passes(0)
+        keep_warm(1)
         regroup_x(0)
         regroup_x(1)
         main_out(0)

@@ -81,9 +81,10 @@ def tile_bottleneck_transformer_pb_s_kernel(
         nc.vector.memset(zeros[:], 0.0)
         warm_bank = psum.tile([P, WARM], F32, tag="f1", name="warm_bank")
 
-        def keep_warm(n):
-            for i in range(n):
-                nc.tensor.matmul(warm_bank[:], lhsT=zeros[:, 0:P], rhs=zeros[:], start=True, stop=True)
+        def keep_warm(columns):
+            nc.tensor.matmul(
+                warm_bank[:, 0:columns], lhsT=zeros[:, 0:P], rhs=zeros[:, 0:columns], start=True, stop=True
+            )
 
         pieces = {}
         stationary = {}
@@ -178,9 +179,10 @@ def tile_bottleneck_transformer_pb_s_kernel(
         def regroup_x(g):
             nc.vector.tensor_copy(out=x_grouped[:, g, :, :, :], in_=x_raw[g][:].rearrange("p b t n -> p b n t"))
 
-        keep_warm(2)
+        keep_warm(WARM)
+        keep_warm(WARM)
         transpose_piece("c3a")
-        keep_warm(1)
+        keep_warm(WARM // 2)
         nc.vector.tensor_copy(out=h_grouped[:], in_=h_raw[:].rearrange("p b t n -> p b n t"))
         std = keep.tile([P, 2, R], F32)
         nc.scalar.activation(out=std[:], in_=v_both, func=ACT.Sqrt, bias=eps[:])
@@ -193,8 +195,9 @@ def tile_bottleneck_transformer_pb_s_kernel(
         scale_both = keep.tile([P, 2, R], F32)
         nc.vector.tensor_tensor(out=scale_both[:], in0=g_both, in1=rstd[:], op=ALU.mult)
         transpose_piece("c3b")
+        keep_warm(WARM // 2)
         main_passes(0)
-        keep_warm(1)
+        keep_warm(WARM // 2)
         regroup_x(0)
         regroup_x(1)
         main_out(0)
@@ -203,8 +206,10 @@ def tile_bottleneck_transformer_pb_s_kernel(
         nc.vector.quantize_mx(
             out=x_codes[:].bitcast(FP8X4), scales=x_scales[:], in_=x_grouped[:].rearrange("p g b n t -> p (g b n t)")
         )
-        for name in ("sc0", "sc1", "sc2", "sc3a", "sc3b"):
+        for name, columns in (("sc0", WARM // 2), ("sc1", WARM // 2), ("sc2", WARM // 4), ("sc3a", 0), ("sc3b", 0)):
             transpose_piece(name)
+            if columns:
+                keep_warm(columns)
         main_passes(1)
         main_out(2)
         main_out(3)

@@ -176,14 +176,22 @@ def tile_bottleneck_transformer_pb_s_kernel(
             nc.scalar.activation(out=result[:, r, :], in_=summed[:, r, :], func=ACT.Relu, bias=shift[:, r : r + 1])
             nc.sync.dma_start(out=out_by_r[r], in_=result[:, r, :].rearrange("p (b n) -> p b n", b=BATCH))
 
+        RUN = 4
+
+        def regroup(grouped, raw):
+            nc.vector.tensor_copy(
+                out=grouped.rearrange("p b (c i) t -> p b c t i", i=RUN),
+                in_=raw[:].rearrange("p b t (c i) -> p b c t i", i=RUN),
+            )
+
         def regroup_x(g):
-            nc.vector.tensor_copy(out=x_grouped[:, g, :, :, :], in_=x_raw[g][:].rearrange("p b t n -> p b n t"))
+            regroup(x_grouped[:, g, :, :, :], x_raw[g])
 
         keep_warm(WARM)
         keep_warm(WARM)
         transpose_piece("c3a")
         keep_warm(WARM // 2)
-        nc.vector.tensor_copy(out=h_grouped[:], in_=h_raw[:].rearrange("p b t n -> p b n t"))
+        regroup(h_grouped[:], h_raw)
         std = keep.tile([P, 2, R], F32)
         nc.scalar.activation(out=std[:], in_=v_both, func=ACT.Sqrt, bias=eps[:])
         nc.vector.quantize_mx(

@@ -36,16 +36,16 @@ def tile_bottleneck_transformer_pb_s_kernel(
         sc3_raw = [keep.tile([P, K_PASS], BF16, name="sc3_raw%d" % g) for g in range(2)]
         h_raw = keep.tile([P, BATCH, PACK, POS], BF16)
         x_raw = [keep.tile([P, BATCH, PACK, POS], BF16, name="x_raw%d" % g) for g in range(2)]
-        vectors = [bn3_v, scbn_v, bn3_g, scbn_g, scbn_m, sc_b, bn3_m, bn3_b, scbn_b]
-        vec_raw = keep.tile([P, len(vectors), 16], BF16)
-        v_both = vec_raw[:, 0:2, 0:R]
-        g_both = vec_raw[:, 2:4, 0:R]
-        msc, csc, m3, b3, bsc = [vec_raw[:, i, 0:R] for i in range(4, len(vectors))]
-        EARLY = 4
-
-        def load_vectors(queue, first, last):
-            for i in range(first, last):
-                queue.dma_start(out=vec_raw[:, i, 0:R], in_=vectors[i].rearrange("(p r) -> p r", r=R))
+        early = [bn3_v, scbn_v, bn3_g, scbn_g]
+        COPIES = 8
+        vec_rows = keep.tile([P, COUT], BF16)
+        vec_words = keep.tile([P, len(early), 2], F32)
+        vec_cols = vec_words[:].rearrange("p j u -> p (j u)").bitcast(BF16).rearrange("p (j r) -> p j r", r=R)
+        v_both = vec_cols[:, 0:2, :]
+        g_both = vec_cols[:, 2:4, :]
+        late = [scbn_m, sc_b, bn3_m, bn3_b, scbn_b]
+        vec_raw = keep.tile([P, len(late), 16], BF16)
+        msc, csc, m3, b3, bsc = [vec_raw[:, i, 0:R] for i in range(len(late))]
 
         def load_x(g):
             nc.sync.dma_start(
@@ -53,7 +53,11 @@ def tile_bottleneck_transformer_pb_s_kernel(
                 in_=x[:, g * K_PASS : (g + 1) * K_PASS, :].rearrange("b (p t) n -> p b (t n)", t=PACK),
             )
 
-        load_vectors(nc.scalar, 0, EARLY)
+        for i, vector in enumerate(early):
+            nc.scalar.dma_start(
+                out=vec_rows[i * COPIES : (i + 1) * COPIES, :], in_=vector.partition_broadcast(COPIES)
+            )
+        filled = len(early) * COPIES
         nc.sync.dma_start(out=conv3_raw[0][:], in_=conv3_rows[:, 0:2, :])
         nc.sync.dma_start(
             out=h_raw[:].rearrange("p b t n -> p b (t n)"), in_=h_attn.rearrange("b (p t) n -> p b (t n)", t=PACK)
@@ -65,7 +69,8 @@ def tile_bottleneck_transformer_pb_s_kernel(
             nc.sync.dma_start(out=sc_raw[r][:], in_=sc_rows[:, r, :])
         for g in range(2):
             nc.sync.dma_start(out=sc3_raw[g][:], in_=sc_rows[:, 3, g * K_PASS : (g + 1) * K_PASS])
-        load_vectors(nc.sync, EARLY, len(vectors))
+        for i, vector in enumerate(late):
+            nc.sync.dma_start(out=vec_raw[:, i, 0:R], in_=vector.rearrange("(p r) -> p r", r=R))
 
         identity = keep.tile([P, P], F32)
         make_identity(nc, identity[:])
@@ -74,11 +79,13 @@ def tile_bottleneck_transformer_pb_s_kernel(
         eps = keep.tile([P, 1], F32)
         nc.vector.memset(eps[:], EPS)
         one_root = keep.tile([P, 1], F32)
-        nc.scalar.activation(out=one_root[:], in_=one[:], func=ACT.Sqrt)
+        nc.scalar.activation(out=one_root[:], in_=one[:], func=ACT.Abs_reciprocal_sqrt)
 
         WARM = 256
         zeros = keep.tile([P, WARM], F32)
         nc.vector.memset(zeros[:], 0.0)
+        nc.vector.memset(vec_rows[filled : 2 * filled, :].bitcast(F32), 0.0)
+        nc.vector.memset(vec_rows[2 * filled : P, :].bitcast(F32), 0.0)
         warm_bank = psum.tile([P, WARM], F32, tag="f1", name="warm_bank")
 
         def keep_warm(columns):
@@ -192,17 +199,20 @@ def tile_bottleneck_transformer_pb_s_kernel(
         transpose_piece("c3a")
         keep_warm(WARM // 2)
         regroup(h_grouped[:], h_raw)
-        std = keep.tile([P, 2, R], F32)
-        nc.scalar.activation(out=std[:], in_=v_both, func=ACT.Sqrt, bias=eps[:])
         nc.vector.quantize_mx(
             out=h_codes[:].bitcast(FP8X4), scales=h_scales[:], in_=h_grouped[:].rearrange("p b n t -> p (b n t)")
         )
         quantise_piece("c3a")
-        rstd = keep.tile([P, 2, R], F32)
-        nc.vector.reciprocal(out=rstd[:], in_=std[:])
-        scale_both = keep.tile([P, 2, R], F32)
-        nc.vector.tensor_tensor(out=scale_both[:], in0=g_both, in1=rstd[:], op=ALU.mult)
         transpose_piece("c3b")
+        row_words = vec_rows[:].bitcast(F32).rearrange("p (q u) -> p u q", u=2)
+        vec_bank = psum.tile([P, 2, P], F32, tag="f0", name="vec_bank")
+        for u in range(2):
+            nc.tensor.transpose(vec_bank[:, u, :], row_words[:, u, :], identity[:])
+        nc.scalar.copy(out=vec_words[:], in_=vec_bank[:, :, 0:filled:COPIES].rearrange("p u j -> p j u"))
+        rstd = keep.tile([P, 2, R], F32)
+        nc.scalar.activation(out=rstd[:], in_=v_both, func=ACT.Abs_reciprocal_sqrt, bias=eps[:])
+        scale_both = keep.tile([P, 2, R], F32)
+        nc.gpsimd.tensor_tensor(out=scale_both[:], in0=g_both, in1=rstd[:], op=ALU.mult)
         keep_warm(WARM // 2)
         main_passes(0)
         keep_warm(WARM // 2)

@@ -197,7 +197,7 @@ def tile_bottleneck_transformer_pb_s_kernel(
         keep_warm(WARM)
         keep_warm(WARM)
         transpose_piece("c3a")
-        keep_warm(WARM // 2)
+        keep_warm(WARM)
         regroup(h_grouped[:], h_raw)
         nc.vector.quantize_mx(
             out=h_codes[:].bitcast(FP8X4), scales=h_scales[:], in_=h_grouped[:].rearrange("p b n t -> p (b n t)")
@@ -215,7 +215,11 @@ def tile_bottleneck_transformer_pb_s_kernel(
         nc.gpsimd.tensor_tensor(out=scale_both[:], in0=g_both, in1=rstd[:], op=ALU.mult)
         keep_warm(WARM // 2)
         main_passes(0)
-        keep_warm(WARM // 2)
+        for v in range(2):
+            nc.tensor.matmul_mx(
+                out=warm_bank[:], rhs=h_codes[:].bitcast(FP8X4), rhs_scale=h_scales[:], start=True, stop=True,
+                **stationary[("main", v, 0)]
+            )
         regroup_x(0)
         regroup_x(1)
         main_out(0)

import concourse.mybir as mybir
from concourse.masks import make_identity

F32 = mybir.dt.float32
BF16 = mybir.dt.bfloat16
U32 = mybir.dt.uint32
U8 = mybir.dt.uint8
FP8X4 = mybir.dt.float8_e4m3fn_x4
ALU = mybir.AluOpType
ACT = mybir.ActivationFunctionType

P = 128
BATCH = 2
POS = 128
COLS = BATCH * POS
COUT = 512
K_MAIN = 512
K_SHORT = 1024
PACK = 4
K_PASS = P * PACK
R = COUT // P
EPS = 1e-5

FLOPS = 2 * BATCH * POS * COUT * (K_MAIN + K_SHORT)


def tile_bottleneck_transformer_pb_s_kernel(
    tc, h_attn, x, conv3_w, bn3_g, bn3_b, bn3_m, bn3_v, sc_w, sc_b, scbn_g, scbn_b, scbn_m, scbn_v, out
):
    nc = tc.nc
    with tc.tile_pool(name="keep", bufs=1) as keep, tc.psum_pool(name="psum", bufs=1) as psum, tc.manual_schedule():
        conv3_rows = conv3_w.rearrange("(p r) k -> p r k", r=R)
        sc_rows = sc_w.rearrange("(p r) k -> p r k", r=R)
        conv3_raw = [keep.tile([P, 2, K_MAIN], BF16, name="conv3_raw%d" % j) for j in range(2)]
        sc_raw = [keep.tile([P, K_SHORT], BF16, name="sc_raw%d" % r) for r in range(R - 1)]
        sc3_raw = [keep.tile([P, K_PASS], BF16, name="sc3_raw%d" % g) for g in range(2)]
        h_raw = keep.tile([P, BATCH, PACK, POS], BF16)
        x_raw = [keep.tile([P, BATCH, PACK, POS], BF16, name="x_raw%d" % g) for g in range(2)]
        early = [bn3_v, scbn_v, bn3_g, scbn_g]
        COPIES = 8
        vec_rows = keep.tile([P, COUT], BF16)
        vec_words = keep.tile([P, len(early), 2], F32)
        vec_cols = vec_words[:].rearrange("p j u -> p (j u)").bitcast(BF16).rearrange("p (j r) -> p j r", r=R)
        v_both = vec_cols[:, 0:2, :]
        g_both = vec_cols[:, 2:4, :]
        late = [scbn_m, sc_b, bn3_m, bn3_b, scbn_b]
        vec_raw = keep.tile([P, len(late), 16], BF16)
        msc, csc, m3, b3, bsc = [vec_raw[:, i, 0:R] for i in range(len(late))]

        def load_x(g):
            nc.sync.dma_start(
                out=x_raw[g][:].rearrange("p b t n -> p b (t n)"),
                in_=x[:, g * K_PASS : (g + 1) * K_PASS, :].rearrange("b (p t) n -> p b (t n)", t=PACK),
            )

        for i, vector in enumerate(early):
            nc.scalar.dma_start(
                out=vec_rows[i * COPIES : (i + 1) * COPIES, :], in_=vector.partition_broadcast(COPIES)
            )
        filled = len(early) * COPIES
        nc.sync.dma_start(out=conv3_raw[0][:], in_=conv3_rows[:, 0:2, :])
        nc.sync.dma_start(
            out=h_raw[:].rearrange("p b t n -> p b (t n)"), in_=h_attn.rearrange("b (p t) n -> p b (t n)", t=PACK)
        )
        nc.sync.dma_start(out=conv3_raw[1][:], in_=conv3_rows[:, 2:4, :])
        load_x(0)
        load_x(1)
        for r in range(R - 1):
            nc.sync.dma_start(out=sc_raw[r][:], in_=sc_rows[:, r, :])
        for g in range(2):
            nc.sync.dma_start(out=sc3_raw[g][:], in_=sc_rows[:, 3, g * K_PASS : (g + 1) * K_PASS])
        for i, vector in enumerate(late):
            nc.sync.dma_start(out=vec_raw[:, i, 0:R], in_=vector.rearrange("(p r) -> p r", r=R))

        identity = keep.tile([P, P], F32)
        make_identity(nc, identity[:])
        one = keep.tile([P, 1], F32)
        nc.vector.memset(one[:], 1.0)
        eps = keep.tile([P, 1], F32)
        nc.vector.memset(eps[:], EPS)
        one_root = keep.tile([P, 1], F32)
        nc.scalar.activation(out=one_root[:], in_=one[:], func=ACT.Abs_reciprocal_sqrt)

        WARM = 256
        zeros = keep.tile([P, WARM], F32)
        nc.vector.memset(zeros[:], 0.0)
        nc.vector.memset(vec_rows[filled : 2 * filled, :].bitcast(F32), 0.0)
        nc.vector.memset(vec_rows[2 * filled : P, :].bitcast(F32), 0.0)
        warm_bank = psum.tile([P, WARM], F32, tag="f1", name="warm_bank")

        def keep_warm(columns):
            nc.tensor.matmul(
                warm_bank[:, 0:columns], lhsT=zeros[:, 0:P], rhs=zeros[:, 0:columns], start=True, stop=True
            )

        pieces = {}
        stationary = {}

        def new_piece(name, raw, keys, bank):
            units = len(keys)
            grouped = keep.tile([P, units * K_PASS], BF16, name="w_grouped_" + name, align_bytes=64)
            codes = keep.tile([P, units * P], U32, name="w_codes_" + name, align_bytes=64)
            scales = keep.tile([P, units * P], U8, name="w_scales_" + name, align_bytes=64)
            for v, key in enumerate(keys):
                cols = slice(v * P, (v + 1) * P)
                stationary[key] = {"lhsT": codes[:, cols].bitcast(FP8X4), "lhsT_scale": scales[:, cols]}
            pieces[name] = (raw, units, grouped, codes, scales, bank)

        new_piece("c3a", conv3_raw[0][:].rearrange("p r k -> p (r k)"), [("main", 0, 0), ("main", 1, 0)], "t0")
        new_piece("c3b", conv3_raw[1][:].rearrange("p r k -> p (r k)"), [("main", 2, 0), ("main", 3, 0)], "t1")
        new_piece("sc0", sc_raw[0][:], [("short", 0, 0), ("short", 0, 1)], "t2")
        new_piece("sc1", sc_raw[1][:], [("short", 1, 0), ("short", 1, 1)], "t3")
        new_piece("sc2", sc_raw[2][:], [("short", 2, 0), ("short", 2, 1)], "t0")
        new_piece("sc3a", sc3_raw[0][:], [("short", 3, 0)], "t1")
        new_piece("sc3b", sc3_raw[1][:], [("short", 3, 1)], "t2")

        def transpose_piece(name):
            raw, units, grouped, codes, scales, bank_tag = pieces[name]
            words = raw.bitcast(F32).rearrange("p (v q u) -> p v u q", v=units, u=2)
            bank = psum.tile([P, units, 2, P], F32, tag=bank_tag, name="bank_" + name)
            for v in range(units):
                for u in range(2):
                    nc.tensor.transpose(bank[:, v, u, :], words[:, v, u, :], identity[:])
            nc.scalar.copy(
                out=grouped[:].bitcast(F32).rearrange("p (v c u) -> p v c u", v=units, u=2),
                in_=bank[:].rearrange("p v u c -> p v c u"),
            )

        def quantise_piece(name):
            raw, units, grouped, codes, scales, bank_tag = pieces[name]
            nc.vector.quantize_mx(out=codes[:].bitcast(FP8X4), scales=scales[:], in_=grouped[:])

        h_grouped = keep.tile([P, BATCH, POS, PACK], BF16, align_bytes=64)
        h_codes = keep.tile([P, COLS], U32, align_bytes=64)
        h_scales = keep.tile([P, COLS], U8, align_bytes=64)
        x_grouped = keep.tile([P, 2, BATCH, POS, PACK], BF16, align_bytes=64)
        x_codes = keep.tile([P, 2 * COLS], U32, align_bytes=64)
        x_scales = keep.tile([P, 2 * COLS], U8, align_bytes=64)
        main_term = keep.tile([P, R, COLS], F32)
        summed = keep.tile([P, R, COLS], F32)
        result = keep.tile([P, R, COLS], F32)
        out_by_r = out.rearrange("b (p r) n -> r p b n", r=R)

        def small(name, width=R):
            return keep.tile([P, width], F32, name=name)

        main_banks = {}

        def main_passes(j):
            bank = psum.tile([P, 2, COLS], F32, tag="m%d" % j, name="main_bank%d" % j)
            main_banks[j] = bank
            for v in range(2):
                nc.tensor.matmul_mx(
                    out=bank[:, v, :], rhs=h_codes[:].bitcast(FP8X4), rhs_scale=h_scales[:], start=True, stop=True,
                    **stationary[("main", 2 * j + v, 0)]
                )

        def main_out(r):
            nc.scalar.activation(
                out=main_term[:, r, :], in_=main_banks[r // 2][:, r % 2, :], func=ACT.Identity,
                scale=scale_both[:, 0, r : r + 1],
            )

        short_banks = {}

        def short_passes(r, bank_tag):
            bank = psum.tile([P, COLS], F32, tag=bank_tag, name="short_bank%d" % r)
            short_banks[r] = bank
            for g in range(2):
                cols = slice(g * COLS, (g + 1) * COLS)
                nc.tensor.matmul_mx(
                    out=bank[:], rhs=x_codes[:, cols].bitcast(FP8X4), rhs_scale=x_scales[:, cols],
                    start=(g == 0), stop=(g == 1), **stationary[("short", r, g)]
                )

        def add_branches(r):
            nc.vector.scalar_tensor_tensor(
                out=summed[:, r, :], in0=short_banks[r][:], scalar=scale_both[:, 1, r : r + 1], in1=main_term[:, r, :],
                op0=ALU.mult, op1=ALU.add,
            )

        def finish(r):
            nc.scalar.activation(out=result[:, r, :], in_=summed[:, r, :], func=ACT.Relu, bias=shift[:, r : r + 1])
            nc.sync.dma_start(out=out_by_r[r], in_=result[:, r, :].rearrange("p (b n) -> p b n", b=BATCH))

        RUN = 4

        def regroup(grouped, raw):
            nc.vector.tensor_copy(
                out=grouped.rearrange("p b (c i) t -> p b c t i", i=RUN),
                in_=raw[:].rearrange("p b t (c i) -> p b c t i", i=RUN),
            )

        def regroup_x(g):
            regroup(x_grouped[:, g, :, :, :], x_raw[g])

        keep_warm(WARM)
        keep_warm(WARM)
        transpose_piece("c3a")
        keep_warm(WARM)
        regroup(h_grouped[:], h_raw)
        nc.vector.quantize_mx(
            out=h_codes[:].bitcast(FP8X4), scales=h_scales[:], in_=h_grouped[:].rearrange("p b n t -> p (b n t)")
        )
        quantise_piece("c3a")
        transpose_piece("c3b")
        row_words = vec_rows[:].bitcast(F32).rearrange("p (q u) -> p u q", u=2)
        vec_bank = psum.tile([P, 2, P], F32, tag="f0", name="vec_bank")
        for u in range(2):
            nc.tensor.transpose(vec_bank[:, u, :], row_words[:, u, :], identity[:])
        nc.scalar.copy(out=vec_words[:], in_=vec_bank[:, :, 0:filled:COPIES].rearrange("p u j -> p j u"))
        rstd = keep.tile([P, 2, R], F32)
        nc.scalar.activation(out=rstd[:], in_=v_both, func=ACT.Abs_reciprocal_sqrt, bias=eps[:])
        scale_both = keep.tile([P, 2, R], F32)
        nc.gpsimd.tensor_tensor(out=scale_both[:], in0=g_both, in1=rstd[:], op=ALU.mult)
        keep_warm(WARM // 2)
        main_passes(0)
        for v in range(2):
            nc.tensor.matmul_mx(
                out=warm_bank[:], rhs=h_codes[:].bitcast(FP8X4), rhs_scale=h_scales[:], start=True, stop=True,
                **stationary[("main", v, 0)]
            )
        regroup_x(0)
        regroup_x(1)
        main_out(0)
        main_out(1)
        quantise_piece("c3b")
        nc.vector.quantize_mx(
            out=x_codes[:].bitcast(FP8X4), scales=x_scales[:], in_=x_grouped[:].rearrange("p g b n t -> p (g b n t)")
        )
        for name, columns in (("sc0", WARM // 2), ("sc1", WARM // 2), ("sc2", WARM // 4), ("sc3a", 0), ("sc3b", 0)):
            transpose_piece(name)
            if columns:
                keep_warm(columns)
        main_passes(1)
        main_out(2)
        main_out(3)
        quantise_piece("sc0")
        short_passes(0, "f0")
        quantise_piece("sc1")
        short_passes(1, "f1")
        mean_less_bias = small("mean_less_bias")
        nc.gpsimd.tensor_tensor(out=mean_less_bias[:], in0=msc, in1=csc, op=ALU.subtract)
        scaled_sc = small("scaled_sc")
        nc.gpsimd.tensor_tensor(out=scaled_sc[:], in0=mean_less_bias[:], in1=scale_both[:, 1, :], op=ALU.mult)
        scaled_3 = small("scaled_3")
        nc.gpsimd.tensor_tensor(out=scaled_3[:], in0=m3, in1=scale_both[:, 0, :], op=ALU.mult)
        shift_3 = small("shift_3")
        nc.gpsimd.tensor_tensor(out=shift_3[:], in0=b3, in1=scaled_3[:], op=ALU.subtract)
        shift_less = small("shift_less")
        nc.gpsimd.tensor_tensor(out=shift_less[:], in0=shift_3[:], in1=scaled_sc[:], op=ALU.subtract)
        shift = small("shift")
        nc.gpsimd.tensor_tensor(out=shift[:], in0=bsc, in1=shift_less[:], op=ALU.add)
        quantise_piece("sc2")
        short_passes(2, "t3")
        quantise_piece("sc3a")
        quantise_piece("sc3b")
        short_passes(3, "m0")
        for r in range(R):
            add_branches(r)
            finish(r)
